import numpy as np
import ml_dtypes

BF16 = ml_dtypes.bfloat16


def bf(x):
    return np.asarray(x, np.float32).astype(BF16)


def f32(x):
    return np.asarray(x, np.float32)


def f64(x):
    return np.asarray(x).astype(np.float64)


def striped(idx):
    return np.tile(idx.reshape(-1, 16).T, (8, 1))


C, S, N, GS = 128, 512, 384, 8


def setup_inputs():
    return {"base": f32(np.random.uniform(0.0, 2.0 / GS, (C, S))), "rates": f32(np.random.uniform(0.05, 1.0, (C, N))), "offs": striped(np.random.permutation(S)[:N])}


def reference(base, rates, offs):
    idx = offs[:16].T.reshape(-1)
    r = f64(rates).reshape(C, N // GS, GS)
    norm = (r / r.sum(axis=-1, keepdims=True)).reshape(C, N)
    out = f64(base).copy()
    out[:, idx] = norm
    return out

@@ -1,0 +1,40 @@
+import concourse.mybir as mybir
+
+F32 = mybir.dt.float32
+U16 = mybir.dt.uint16
+
+SAMPLES = 128
+NEURONS = 512
+LISTED = 384
+POOL = 8
+POOLS = LISTED // POOL
+
+
+def tile_lateral_layer_kernel(tc, base, rates, offs, out):
+    nc = tc.nc
+    with tc.tile_pool(name="held", bufs=1) as held:
+        offsets = held.tile([SAMPLES, LISTED // 16], U16, name="offsets")
+        window = held.tile([SAMPLES, NEURONS], F32, name="window")
+        rate = held.tile([SAMPLES, LISTED], F32, name="rate")
+        pool_sum = held.tile([SAMPLES, POOLS], F32, name="pool_sum")
+        pool_inv = held.tile([SAMPLES, POOLS], F32, name="pool_inv")
+        entry_inv = held.tile([SAMPLES, LISTED], F32, name="entry_inv")
+
+        nc.scalar.dma_start(rate[:], rates)
+        nc.sync.dma_start(offsets[:], offs)
+        nc.sync.dma_start(window[:], base)
+
+        by_pool = rate[:].rearrange("p (g t) -> p g t", t=POOL)
+        nc.vector.reduce_sum(pool_sum[:], by_pool, axis=mybir.AxisListType.X)
+        nc.vector.reciprocal(pool_inv[:], pool_sum[:])
+
+        nc.vector.tensor_copy(
+            entry_inv[:].rearrange("p (g t) -> p g t", t=POOL),
+            pool_inv[:].unsqueeze(2).to_broadcast([SAMPLES, POOLS, POOL]),
+        )
+
+        nc.vector.tensor_tensor(
+            window[:].indirect(offsets[:]), rate[:], entry_inv[:], mybir.AluOpType.mult
+        )
+
+        nc.sync.dma_start(out, window[:])

@@ -37,4 +37,8 @@ def tile_lateral_layer_kernel(tc, base, rates, offs, out):
             window[:].indirect(offsets[:]), rate[:], entry_inv[:], mybir.AluOpType.mult
         )
 
-        nc.sync.dma_start(out, window[:])
+        quarter = NEURONS // 4
+        for q in range(4):
+            queue = nc.sync if q % 2 == 0 else nc.scalar
+            columns = slice(q * quarter, (q + 1) * quarter)
+            queue.dma_start(out[:, columns], window[:, columns])

@@ -8,6 +8,7 @@ NEURONS = 512
 LISTED = 384
 POOL = 8
 POOLS = LISTED // POOL
+FIRST = LISTED // 3
 
 
 def tile_lateral_layer_kernel(tc, base, rates, offs, out):
@@ -18,7 +19,8 @@ def tile_lateral_layer_kernel(tc, base, rates, offs, out):
         rate = held.tile([SAMPLES, LISTED], F32, name="rate")
         pool_sum = held.tile([SAMPLES, POOLS], F32, name="pool_sum")
         pool_inv = held.tile([SAMPLES, POOLS], F32, name="pool_inv")
-        entry_inv = held.tile([SAMPLES, LISTED], F32, name="entry_inv")
+        first_inv = held.tile([SAMPLES, FIRST], F32, name="first_inv")
+        rest_inv = held.tile([SAMPLES, LISTED - FIRST], F32, name="rest_inv")
 
         nc.scalar.dma_start(rate[:], rates)
         nc.sync.dma_start(offsets[:], offs)
@@ -29,16 +31,19 @@ def tile_lateral_layer_kernel(tc, base, rates, offs, out):
         nc.vector.reciprocal(pool_inv[:], pool_sum[:])
 
         nc.vector.tensor_copy(
-            entry_inv[:].rearrange("p (g t) -> p g t", t=POOL),
-            pool_inv[:].unsqueeze(2).to_broadcast([SAMPLES, POOLS, POOL]),
+            first_inv[:].rearrange("p (g t) -> p g t", t=POOL),
+            pool_inv[:, : FIRST // POOL].unsqueeze(2).to_broadcast([SAMPLES, FIRST // POOL, POOL]),
+        )
+        nc.scalar.copy(
+            rest_inv[:].rearrange("p (g t) -> p g t", t=POOL),
+            pool_inv[:, FIRST // POOL :].unsqueeze(2).to_broadcast([SAMPLES, POOLS - FIRST // POOL, POOL]),
         )
 
         nc.vector.tensor_tensor(
-            window[:].indirect(offsets[:]), rate[:], entry_inv[:], mybir.AluOpType.mult
+            window[:].indirect(offsets[:, : FIRST // 16]), rate[:, :FIRST], first_inv[:], mybir.AluOpType.mult
+        )
+        nc.vector.tensor_tensor(
+            window[:].indirect(offsets[:, FIRST // 16 :]), rate[:, FIRST:], rest_inv[:], mybir.AluOpType.mult
         )
 
-        quarter = NEURONS // 4
-        for q in range(4):
-            queue = nc.sync if q % 2 == 0 else nc.scalar
-            columns = slice(q * quarter, (q + 1) * quarter)
-            queue.dma_start(out[:, columns], window[:, columns])
+        nc.sync.dma_start(out, window[:])

@@ -8,7 +8,6 @@ NEURONS = 512
 LISTED = 384
 POOL = 8
 POOLS = LISTED // POOL
-FIRST = LISTED // 3
 
 
 def tile_lateral_layer_kernel(tc, base, rates, offs, out):
@@ -19,10 +18,9 @@ def tile_lateral_layer_kernel(tc, base, rates, offs, out):
         rate = held.tile([SAMPLES, LISTED], F32, name="rate")
         pool_sum = held.tile([SAMPLES, POOLS], F32, name="pool_sum")
         pool_inv = held.tile([SAMPLES, POOLS], F32, name="pool_inv")
-        first_inv = held.tile([SAMPLES, FIRST], F32, name="first_inv")
-        rest_inv = held.tile([SAMPLES, LISTED - FIRST], F32, name="rest_inv")
+        entry_inv = held.tile([SAMPLES, LISTED], F32, name="entry_inv")
 
-        nc.scalar.dma_start(rate[:], rates)
+        nc.sync.dma_start(rate[:], rates)
         nc.sync.dma_start(offsets[:], offs)
         nc.sync.dma_start(window[:], base)
 
@@ -31,19 +29,12 @@ def tile_lateral_layer_kernel(tc, base, rates, offs, out):
         nc.vector.reciprocal(pool_inv[:], pool_sum[:])
 
         nc.vector.tensor_copy(
-            first_inv[:].rearrange("p (g t) -> p g t", t=POOL),
-            pool_inv[:, : FIRST // POOL].unsqueeze(2).to_broadcast([SAMPLES, FIRST // POOL, POOL]),
-        )
-        nc.scalar.copy(
-            rest_inv[:].rearrange("p (g t) -> p g t", t=POOL),
-            pool_inv[:, FIRST // POOL :].unsqueeze(2).to_broadcast([SAMPLES, POOLS - FIRST // POOL, POOL]),
+            entry_inv[:].rearrange("p (g t) -> p g t", t=POOL),
+            pool_inv[:].unsqueeze(2).to_broadcast([SAMPLES, POOLS, POOL]),
         )
 
         nc.vector.tensor_tensor(
-            window[:].indirect(offsets[:, : FIRST // 16]), rate[:, :FIRST], first_inv[:], mybir.AluOpType.mult
-        )
-        nc.vector.tensor_tensor(
-            window[:].indirect(offsets[:, FIRST // 16 :]), rate[:, FIRST:], rest_inv[:], mybir.AluOpType.mult
+            window[:].indirect(offsets[:]), rate[:], entry_inv[:], mybir.AluOpType.mult
         )
 
         nc.sync.dma_start(out, window[:])

@@ -8,6 +8,9 @@ NEURONS = 512
 LISTED = 384
 POOL = 8
 POOLS = LISTED // POOL
+CHUNKS = 2
+CHUNK = LISTED // CHUNKS
+CHUNK_POOLS = CHUNK // POOL
 
 
 def tile_lateral_layer_kernel(tc, base, rates, offs, out):
@@ -20,18 +23,33 @@ def tile_lateral_layer_kernel(tc, base, rates, offs, out):
         pool_inv = held.tile([SAMPLES, POOLS], F32, name="pool_inv")
         entry_inv = held.tile([SAMPLES, LISTED], F32, name="entry_inv")
 
-        nc.sync.dma_start(rate[:], rates)
+        for c in range(CHUNKS):
+            columns = slice(c * CHUNK, (c + 1) * CHUNK)
+            nc.sync.dma_start(rate[:, columns], rates[:, columns])
         nc.sync.dma_start(offsets[:], offs)
         nc.sync.dma_start(window[:], base)
 
-        by_pool = rate[:].rearrange("p (g t) -> p g t", t=POOL)
-        nc.vector.reduce_sum(pool_sum[:], by_pool, axis=mybir.AxisListType.X)
-        nc.vector.reciprocal(pool_inv[:], pool_sum[:])
 
-        nc.vector.tensor_copy(
-            entry_inv[:].rearrange("p (g t) -> p g t", t=POOL),
-            pool_inv[:].unsqueeze(2).to_broadcast([SAMPLES, POOLS, POOL]),
-        )
+        for c in range(CHUNKS):
+            columns = slice(c * CHUNK, (c + 1) * CHUNK)
+            pools = slice(c * CHUNK_POOLS, (c + 1) * CHUNK_POOLS)
+            nc.vector.reduce_sum(
+                pool_sum[:, pools],
+                rate[:, columns].rearrange("p (g t) -> p g t", t=POOL),
+                axis=mybir.AxisListType.X,
+            )
+
+        for c in range(CHUNKS):
+            pools = slice(c * CHUNK_POOLS, (c + 1) * CHUNK_POOLS)
+            nc.vector.reciprocal(pool_inv[:, pools], pool_sum[:, pools])
+
+        for c in range(CHUNKS):
+            columns = slice(c * CHUNK, (c + 1) * CHUNK)
+            pools = slice(c * CHUNK_POOLS, (c + 1) * CHUNK_POOLS)
+            nc.vector.tensor_copy(
+                entry_inv[:, columns].rearrange("p (g t) -> p g t", t=POOL),
+                pool_inv[:, pools].unsqueeze(2).to_broadcast([SAMPLES, CHUNK_POOLS, POOL]),
+            )
 
         nc.vector.tensor_tensor(
             window[:].indirect(offsets[:]), rate[:], entry_inv[:], mybir.AluOpType.mult

@@ -8,7 +8,7 @@ NEURONS = 512
 LISTED = 384
 POOL = 8
 POOLS = LISTED // POOL
-CHUNKS = 2
+CHUNKS = 3
 CHUNK = LISTED // CHUNKS
 CHUNK_POOLS = CHUNK // POOL
 
@@ -23,9 +23,7 @@ def tile_lateral_layer_kernel(tc, base, rates, offs, out):
         pool_inv = held.tile([SAMPLES, POOLS], F32, name="pool_inv")
         entry_inv = held.tile([SAMPLES, LISTED], F32, name="entry_inv")
 
-        for c in range(CHUNKS):
-            columns = slice(c * CHUNK, (c + 1) * CHUNK)
-            nc.sync.dma_start(rate[:, columns], rates[:, columns])
+        nc.sync.dma_start(rate[:], rates)
         nc.sync.dma_start(offsets[:], offs)
         nc.sync.dma_start(window[:], base)
 

@@ -24,8 +24,8 @@ def tile_lateral_layer_kernel(tc, base, rates, offs, out):
         entry_inv = held.tile([SAMPLES, LISTED], F32, name="entry_inv")
 
         nc.sync.dma_start(rate[:], rates)
-        nc.sync.dma_start(offsets[:], offs)
         nc.sync.dma_start(window[:], base)
+        nc.sync.dma_start(offsets[:], offs)
 
 
         for c in range(CHUNKS):

@@ -8,6 +8,7 @@ NEURONS = 512
 LISTED = 384
 POOL = 8
 POOLS = LISTED // POOL
+DMA_UNIT = 256
 CHUNKS = 3
 CHUNK = LISTED // CHUNKS
 CHUNK_POOLS = CHUNK // POOL
@@ -17,8 +18,8 @@ def tile_lateral_layer_kernel(tc, base, rates, offs, out):
     nc = tc.nc
     with tc.tile_pool(name="held", bufs=1) as held:
         offsets = held.tile([SAMPLES, LISTED // 16], U16, name="offsets")
-        window = held.tile([SAMPLES, NEURONS], F32, name="window")
-        rate = held.tile([SAMPLES, LISTED], F32, name="rate")
+        window = held.tile([SAMPLES, NEURONS], F32, name="window", align_bytes=DMA_UNIT)
+        rate = held.tile([SAMPLES, LISTED], F32, name="rate", align_bytes=DMA_UNIT)
         pool_sum = held.tile([SAMPLES, POOLS], F32, name="pool_sum")
         pool_inv = held.tile([SAMPLES, POOLS], F32, name="pool_inv")
         entry_inv = held.tile([SAMPLES, LISTED], F32, name="entry_inv")

@@ -9,7 +9,7 @@ LISTED = 384
 POOL = 8
 POOLS = LISTED // POOL
 DMA_UNIT = 256
-CHUNKS = 3
+CHUNKS = 4
 CHUNK = LISTED // CHUNKS
 CHUNK_POOLS = CHUNK // POOL
 

import concourse.mybir as mybir

F32 = mybir.dt.float32
U16 = mybir.dt.uint16

SAMPLES = 128
NEURONS = 512
LISTED = 384
POOL = 8
POOLS = LISTED // POOL
DMA_UNIT = 256
CHUNKS = 4
CHUNK = LISTED // CHUNKS
CHUNK_POOLS = CHUNK // POOL


def tile_lateral_layer_kernel(tc, base, rates, offs, out):
    nc = tc.nc
    with tc.tile_pool(name="held", bufs=1) as held:
        offsets = held.tile([SAMPLES, LISTED // 16], U16, name="offsets")
        window = held.tile([SAMPLES, NEURONS], F32, name="window", align_bytes=DMA_UNIT)
        rate = held.tile([SAMPLES, LISTED], F32, name="rate", align_bytes=DMA_UNIT)
        pool_sum = held.tile([SAMPLES, POOLS], F32, name="pool_sum")
        pool_inv = held.tile([SAMPLES, POOLS], F32, name="pool_inv")
        entry_inv = held.tile([SAMPLES, LISTED], F32, name="entry_inv")

        nc.sync.dma_start(rate[:], rates)
        nc.sync.dma_start(window[:], base)
        nc.sync.dma_start(offsets[:], offs)


        for c in range(CHUNKS):
            columns = slice(c * CHUNK, (c + 1) * CHUNK)
            pools = slice(c * CHUNK_POOLS, (c + 1) * CHUNK_POOLS)
            nc.vector.reduce_sum(
                pool_sum[:, pools],
                rate[:, columns].rearrange("p (g t) -> p g t", t=POOL),
                axis=mybir.AxisListType.X,
            )

        for c in range(CHUNKS):
            pools = slice(c * CHUNK_POOLS, (c + 1) * CHUNK_POOLS)
            nc.vector.reciprocal(pool_inv[:, pools], pool_sum[:, pools])

        for c in range(CHUNKS):
            columns = slice(c * CHUNK, (c + 1) * CHUNK)
            pools = slice(c * CHUNK_POOLS, (c + 1) * CHUNK_POOLS)
            nc.vector.tensor_copy(
                entry_inv[:, columns].rearrange("p (g t) -> p g t", t=POOL),
                pool_inv[:, pools].unsqueeze(2).to_broadcast([SAMPLES, CHUNK_POOLS, POOL]),
            )

        nc.vector.tensor_tensor(
            window[:].indirect(offsets[:]), rate[:], entry_inv[:], mybir.AluOpType.mult
        )

        nc.sync.dma_start(out, window[:])
